import numpy as np
import ml_dtypes


def mxq(x, axis, fmt="e4m3"):
    dtype, down = {"e4m3": (ml_dtypes.float8_e4m3fn, 7), "e5m2": (ml_dtypes.float8_e5m2, 14)}[fmt]
    v = np.moveaxis(np.asarray(x, np.float32).astype(ml_dtypes.bfloat16).astype(np.float64), axis, -1)
    blocks = v.reshape(v.shape[:-1] + (-1, 32))
    amax = np.abs(blocks).max(-1, keepdims=True)
    byte = np.maximum(np.where(amax > 0, np.frexp(amax)[1] - 1 + 127, 0) - down, 1)
    scale = np.exp2(byte - 127.0)
    codes = (blocks / scale).astype(np.float32).astype(dtype).astype(np.float64)
    return np.moveaxis((codes * scale).reshape(v.shape), -1, axis)


WIDE = False


def mx_kscale(k):
    if not WIDE:
        return np.ones(k)
    levels = np.array([10, -10, 5, -5, 0])
    a = np.random.permutation(np.resize(levels, k // 512 * 4)).reshape(k // 512, 4)
    idx = np.arange(k)
    return np.exp2(a[idx // 512, idx % 128 // 32])


BF16 = ml_dtypes.bfloat16


def bf(x):
    return np.asarray(x, np.float32).astype(BF16)


def f64(x):
    return np.asarray(x).astype(np.float64)


B, N, G, L = 1024, 512, 128, 768
N2 = 2 * N


def setup_inputs():
    s = mx_kscale(N2)
    return {
        "Volt": bf(np.random.standard_normal((B, N2)) * s),
        "Y": bf(np.random.standard_normal((N2, N2)) / np.sqrt(N2) / s[None, :] / s[:, None]),
        "Yconj": bf(np.random.standard_normal((N2, N2)) / np.sqrt(N2) / s[None, :] / s[:, None]),
    }


def reference(Volt, Y, Yconj):
    v = f64(Volt)
    vq = mxq(v, 1, "e4m3")
    quad_p = v * (vq @ mxq(f64(Y), 1, "e4m3").T)
    quad_q = v * (vq @ mxq(f64(Yconj), 1, "e4m3").T)
    return quad_p, quad_q

@@ -1,0 +1,199 @@
+from contextlib import ExitStack
+
+import concourse.bass as bass
+import concourse.mybir as mybir
+import concourse.tile as tile
+from concourse.masks import make_identity
+
+F32 = mybir.dt.float32
+BF16 = mybir.dt.bfloat16
+U32 = mybir.dt.uint32
+U8 = mybir.dt.uint8
+FP8X4 = mybir.dt.float8_e4m3fn_x4
+MULT = mybir.AluOpType.mult
+
+P = 128
+K = 1024
+KW = K // 2
+FLOPS = 2 * 2 * 1024 * 1024 * 1024
+
+OFFLOAD = ((1, 1, 0), (1, 3, 0), (1, 5, 0))
+
+
+def tile_pinnlayer_pb_kernel(tc, Volt, Y, Yconj, out_0, out_1):
+    nc = tc.nc
+    mats = (Y, Yconj)
+    out_views = tuple(o.rearrange("(p t) r -> p t r", t=8) for o in (out_0, out_1))
+    volt_view = Volt.rearrange("(p t) k -> p t k", t=8)
+
+    with ExitStack() as ctx:
+        keep = ctx.enter_context(tc.tile_pool(name="keep", bufs=1))
+        tp_pool = ctx.enter_context(tc.psum_pool(name="tp", bufs=4))
+        acc_pool = ctx.enter_context(tc.psum_pool(name="acc", bufs=4))
+        ctx.enter_context(tc.manual_schedule())
+
+        ident = keep.tile([P, P], F32, name="ident")
+        make_identity(nc, ident[:])
+
+        def load(view, rows, name):
+            raw = keep.tile([P, rows * K], BF16, name=name)
+            nc.sync.dma_start(out=raw[:].rearrange("p (t k) -> p t k", t=rows), in_=view)
+            return raw
+
+        def load_half(m, h, pieces):
+            view = mats[m][512 * h : 512 * (h + 1), :].rearrange("(q t) k -> q t k", t=4)
+            per = 4 // pieces
+            chunks = []
+            for s in range(pieces):
+                raw = load(view[:, per * s : per * (s + 1), :], per, "yraw%d%d%d" % (m, h, s))
+                words = raw[:].bitcast(F32)
+                for t in range(per):
+                    chunks.append(words[:, KW * t : KW * (t + 1)])
+            return chunks
+
+        y_chunks = {}
+        v_raw = []
+        y_chunks[(0, 0)] = load_half(0, 0, 2)
+        y_chunks[(0, 1)] = load_half(0, 1, 1)
+        for j in range(4):
+            v_raw.append(load(volt_view[:, 2 * j : 2 * j + 2, :], 2, "vraw%d" % j))
+        y_chunks[(1, 0)] = load_half(1, 0, 1)
+        y_chunks[(1, 1)] = load_half(1, 1, 1)
+
+        y_grp = {}
+        y_codes = {}
+        y_scales = {}
+        for m in range(2):
+            for h in range(2):
+                y_grp[(m, h)] = keep.tile([P, 4096], BF16, name="ygrp%d%d" % (m, h), align_bytes=64)
+                y_codes[(m, h)] = keep.tile([P, 1024], U32, name="ycod%d%d" % (m, h), align_bytes=64)
+                y_scales[(m, h)] = keep.tile([P, 1024], U8, name="yscl%d%d" % (m, h), align_bytes=64)
+        v_grp = []
+        v_codes = []
+        v_scales = []
+        o_sb = {}
+        for j in range(4):
+            v_grp.append(keep.tile([P, 2048], BF16, name="vgrp%d" % j, align_bytes=64))
+            v_codes.append(keep.tile([P, 512], U32, name="vcod%d" % j, align_bytes=64))
+            v_scales.append(keep.tile([P, 512], U8, name="vscl%d" % j, align_bytes=64))
+            for m in range(2):
+                o_sb[(m, j)] = keep.tile([P, 2048], F32, name="osb%d%d" % (m, j))
+
+        def transpose_chunk(words):
+            ps = tp_pool.tile([P, 4, P], F32)
+            for w in range(4):
+                nc.tensor.transpose(ps[:, w, :], words[:, P * w : P * (w + 1)], ident[:])
+            return ps
+
+        def copy_out(on_vector, ps, dest):
+            src = ps[:].rearrange("p (g u) r -> p g r u", g=2)
+            if on_vector:
+                nc.vector.tensor_copy(out=dest, in_=src)
+            else:
+                nc.scalar.copy(out=dest, in_=src)
+
+        def flip_y(m, h, t, on_vector):
+            ps = transpose_chunk(y_chunks[(m, h)][t])
+            dest = y_grp[(m, h)][:].bitcast(F32).rearrange("p (g t q u) -> p g t q u", g=2, t=4, u=2)
+            copy_out(on_vector, ps, dest[:, :, t, :, :])
+
+        def flip_v(i, on_vector):
+            j, c = divmod(i, 2)
+            ps = transpose_chunk(v_raw[j][:].bitcast(F32)[:, KW * c : KW * (c + 1)])
+            dest = v_grp[j][:].bitcast(F32).rearrange("p (c g b u) -> p c g b u", c=2, g=2, u=2)
+            copy_out(on_vector, ps, dest[:, c, :, :, :])
+
+        def quant_y(m, h, g):
+            nc.vector.quantize_mx(
+                out=y_codes[(m, h)][:, 512 * g : 512 * (g + 1)].bitcast(FP8X4),
+                scales=y_scales[(m, h)][:, 512 * g : 512 * (g + 1)],
+                in_=y_grp[(m, h)][:, 2048 * g : 2048 * (g + 1)],
+            )
+
+        def quant_v(j):
+            nc.vector.quantize_mx(out=v_codes[j][:].bitcast(FP8X4), scales=v_scales[j][:], in_=v_grp[j][:])
+
+        def mx_tile(m, i, h):
+            j, c = divmod(i, 2)
+            acc = acc_pool.tile([P, 512], F32)
+            for g in range(2):
+                lo = 256 * c + 128 * g
+                nc.tensor.matmul_mx(
+                    out=acc[:],
+                    lhsT=v_codes[j][:, lo : lo + 128].bitcast(FP8X4),
+                    lhsT_scale=v_scales[j][:, lo : lo + 128],
+                    rhs=y_codes[(m, h)][:, 512 * g : 512 * (g + 1)].bitcast(FP8X4),
+                    rhs_scale=y_scales[(m, h)][:, 512 * g : 512 * (g + 1)],
+                    start=(g == 0),
+                    stop=(g == 1),
+                )
+            return acc
+
+        def product(acc, m, i, h):
+            j, c = divmod(i, 2)
+            lo = 1024 * c + 512 * h
+            dst = o_sb[(m, j)][:, lo : lo + 512]
+            fac = v_raw[j][:, lo : lo + 512]
+            src = acc[:].rearrange("b (t q) -> b q t", t=4)
+            dst3 = dst.rearrange("b (q t) -> b q t", t=4)
+            if (m, i, h) in OFFLOAD:
+                nc.scalar.copy(out=dst3, in_=src)
+                nc.gpsimd.tensor_tensor(out=dst, in0=dst, in1=fac, op=MULT)
+            else:
+                nc.vector.tensor_tensor(out=dst3, in0=src, in1=fac.rearrange("b (q t) -> b q t", t=4), op=MULT)
+
+        def tiles(m, order):
+            for i, h in order:
+                product(mx_tile(m, i, h), m, i, h)
+
+        def pair_order(j):
+            return ((2 * j, 0), (2 * j + 1, 0), (2 * j, 1), (2 * j + 1, 1))
+
+        def store_pair(m, j):
+            nc.sync.dma_start(
+                out=out_views[m][:, 2 * j : 2 * j + 2, :],
+                in_=o_sb[(m, j)][:].rearrange("p (c r) -> p c r", c=2),
+            )
+
+        for h in range(2):
+            for t in range(4):
+                flip_y(0, h, t, t == 3)
+            quant_y(0, h, 0)
+            quant_y(0, h, 1)
+        for j in range(2):
+            flip_v(2 * j, False)
+            flip_v(2 * j + 1, True)
+            quant_v(j)
+
+        tiles(0, pair_order(0))
+        store_pair(0, 0)
+        for i in range(4, 8):
+            flip_v(i, False)
+        quant_v(2)
+        tiles(0, pair_order(1))
+        store_pair(0, 1)
+        for t in range(4):
+            flip_y(1, 0, t, False)
+        quant_v(3)
+        tiles(0, pair_order(2))
+        store_pair(0, 2)
+        for t in range(4):
+            flip_y(1, 1, t, False)
+        quant_y(1, 0, 0)
+        quant_y(1, 0, 1)
+        tiles(0, pair_order(3)[:2])
+        quant_y(1, 1, 0)
+        quant_y(1, 1, 1)
+        tiles(0, pair_order(3)[2:])
+        store_pair(0, 3)
+        for j in range(3):
+            tiles(1, pair_order(j))
+            store_pair(1, j)
+        tiles(1, ((6, 0), (6, 1)))
+        nc.sync.dma_start(out=out_views[1][:, 6, :], in_=o_sb[(1, 3)][:, 0:1024])
+        for h in range(2):
+            tiles(1, ((7, h),))
+            nc.sync.dma_start(
+                out=out_views[1][:, 7, 512 * h : 512 * (h + 1)],
+                in_=o_sb[(1, 3)][:, 1024 + 512 * h : 1024 + 512 * (h + 1)],
+            )

@@ -1,8 +1,6 @@
 from contextlib import ExitStack
 
-import concourse.bass as bass
 import concourse.mybir as mybir
-import concourse.tile as tile
 from concourse.masks import make_identity
 
 F32 = mybir.dt.float32
@@ -17,7 +15,7 @@ K = 1024
 KW = K // 2
 FLOPS = 2 * 2 * 1024 * 1024 * 1024
 
-OFFLOAD = ((1, 1, 0), (1, 3, 0), (1, 5, 0))
+OFFLOAD = ((1, 0, 0), (1, 2, 0), (1, 4, 0), (1, 6, 0))
 
 
 def tile_pinnlayer_pb_kernel(tc, Volt, Y, Yconj, out_0, out_1):
@@ -54,9 +52,9 @@ def tile_pinnlayer_pb_kernel(tc, Volt, Y, Yconj, out_0, out_1):
         y_chunks = {}
         v_raw = []
         y_chunks[(0, 0)] = load_half(0, 0, 2)
-        y_chunks[(0, 1)] = load_half(0, 1, 1)
         for j in range(4):
             v_raw.append(load(volt_view[:, 2 * j : 2 * j + 2, :], 2, "vraw%d" % j))
+        y_chunks[(0, 1)] = load_half(0, 1, 1)
         y_chunks[(1, 0)] = load_half(1, 0, 1)
         y_chunks[(1, 1)] = load_half(1, 1, 1)
 
@@ -65,55 +63,77 @@ def tile_pinnlayer_pb_kernel(tc, Volt, Y, Yconj, out_0, out_1):
         y_scales = {}
         for m in range(2):
             for h in range(2):
-                y_grp[(m, h)] = keep.tile([P, 4096], BF16, name="ygrp%d%d" % (m, h), align_bytes=64)
+                if (m, h) == (0, 0):
+                    for t in range(4):
+                        y_grp[(m, h, t)] = keep.tile([P, 1024], BF16, name="ygrp%d%d%d" % (m, h, t), align_bytes=64)
+                else:
+                    y_grp[(m, h)] = keep.tile([P, 4096], BF16, name="ygrp%d%d" % (m, h), align_bytes=64)
                 y_codes[(m, h)] = keep.tile([P, 1024], U32, name="ycod%d%d" % (m, h), align_bytes=64)
                 y_scales[(m, h)] = keep.tile([P, 1024], U8, name="yscl%d%d" % (m, h), align_bytes=64)
-        v_grp = []
+        v_grp = {}
         v_codes = []
         v_scales = []
         o_sb = {}
+        for i in range(4):
+            v_grp[i] = keep.tile([P, 1024], BF16, name="vgrpc%d" % i, align_bytes=64)
         for j in range(4):
-            v_grp.append(keep.tile([P, 2048], BF16, name="vgrp%d" % j, align_bytes=64))
+            if j >= 2:
+                v_grp[(j,)] = keep.tile([P, 2048], BF16, name="vgrpp%d" % j, align_bytes=64)
             v_codes.append(keep.tile([P, 512], U32, name="vcod%d" % j, align_bytes=64))
             v_scales.append(keep.tile([P, 512], U8, name="vscl%d" % j, align_bytes=64))
             for m in range(2):
                 o_sb[(m, j)] = keep.tile([P, 2048], F32, name="osb%d%d" % (m, j))
 
-        def transpose_chunk(words):
+        def flip(words, dest):
             ps = tp_pool.tile([P, 4, P], F32)
             for w in range(4):
                 nc.tensor.transpose(ps[:, w, :], words[:, P * w : P * (w + 1)], ident[:])
-            return ps
+            nc.scalar.copy(out=dest, in_=ps[:].rearrange("p (g u) r -> p g r u", g=2))
 
-        def copy_out(on_vector, ps, dest):
-            src = ps[:].rearrange("p (g u) r -> p g r u", g=2)
-            if on_vector:
-                nc.vector.tensor_copy(out=dest, in_=src)
+        def flip_y(m, h, t):
+            if (m, h) == (0, 0):
+                dest = y_grp[(m, h, t)][:].bitcast(F32).rearrange("p (g q u) -> p g q u", g=2, u=2)
             else:
-                nc.scalar.copy(out=dest, in_=src)
+                dest = y_grp[(m, h)][:].bitcast(F32).rearrange("p (g t q u) -> p g t q u", g=2, t=4, u=2)[:, :, t, :, :]
+            flip(y_chunks[(m, h)][t], dest)
 
-        def flip_y(m, h, t, on_vector):
-            ps = transpose_chunk(y_chunks[(m, h)][t])
-            dest = y_grp[(m, h)][:].bitcast(F32).rearrange("p (g t q u) -> p g t q u", g=2, t=4, u=2)
-            copy_out(on_vector, ps, dest[:, :, t, :, :])
-
-        def flip_v(i, on_vector):
+        def flip_v(i):
             j, c = divmod(i, 2)
-            ps = transpose_chunk(v_raw[j][:].bitcast(F32)[:, KW * c : KW * (c + 1)])
-            dest = v_grp[j][:].bitcast(F32).rearrange("p (c g b u) -> p c g b u", c=2, g=2, u=2)
-            copy_out(on_vector, ps, dest[:, c, :, :, :])
+            if i < 4:
+                dest = v_grp[i][:].bitcast(F32).rearrange("p (g b u) -> p g b u", g=2, u=2)
+            else:
+                dest = v_grp[(j,)][:].bitcast(F32).rearrange("p (c g b u) -> p c g b u", c=2, g=2, u=2)[:, c, :, :, :]
+            flip(v_raw[j][:].bitcast(F32)[:, KW * c : KW * (c + 1)], dest)
 
-        def quant_y(m, h, g):
+        def quant_y_chunk(t):
+            for g in range(2):
+                lo = 512 * g + 128 * t
+                nc.vector.quantize_mx(
+                    out=y_codes[(0, 0)][:, lo : lo + 128].bitcast(FP8X4),
+                    scales=y_scales[(0, 0)][:, lo : lo + 128],
+                    in_=y_grp[(0, 0, t)][:, 512 * g : 512 * (g + 1)],
+                )
+
+        def quant_y(m, h):
+            for g in range(2):
+                nc.vector.quantize_mx(
+                    out=y_codes[(m, h)][:, 512 * g : 512 * (g + 1)].bitcast(FP8X4),
+                    scales=y_scales[(m, h)][:, 512 * g : 512 * (g + 1)],
+                    in_=y_grp[(m, h)][:, 2048 * g : 2048 * (g + 1)],
+                )
+
+        def quant_v_chunk(i):
+            j, c = divmod(i, 2)
             nc.vector.quantize_mx(
-                out=y_codes[(m, h)][:, 512 * g : 512 * (g + 1)].bitcast(FP8X4),
-                scales=y_scales[(m, h)][:, 512 * g : 512 * (g + 1)],
-                in_=y_grp[(m, h)][:, 2048 * g : 2048 * (g + 1)],
+                out=v_codes[j][:, 256 * c : 256 * (c + 1)].bitcast(FP8X4),
+                scales=v_scales[j][:, 256 * c : 256 * (c + 1)],
+                in_=v_grp[i][:],
             )
 
-        def quant_v(j):
-            nc.vector.quantize_mx(out=v_codes[j][:].bitcast(FP8X4), scales=v_scales[j][:], in_=v_grp[j][:])
+        def quant_v_pair(j):
+            nc.vector.quantize_mx(out=v_codes[j][:].bitcast(FP8X4), scales=v_scales[j][:], in_=v_grp[(j,)][:])
 
-        def mx_tile(m, i, h):
+        def tile_out(m, i, h):
             j, c = divmod(i, 2)
             acc = acc_pool.tile([P, 512], F32)
             for g in range(2):
@@ -127,10 +147,6 @@ def tile_pinnlayer_pb_kernel(tc, Volt, Y, Yconj, out_0, out_1):
                     start=(g == 0),
                     stop=(g == 1),
                 )
-            return acc
-
-        def product(acc, m, i, h):
-            j, c = divmod(i, 2)
             lo = 1024 * c + 512 * h
             dst = o_sb[(m, j)][:, lo : lo + 512]
             fac = v_raw[j][:, lo : lo + 512]
@@ -142,58 +158,72 @@ def tile_pinnlayer_pb_kernel(tc, Volt, Y, Yconj, out_0, out_1):
             else:
                 nc.vector.tensor_tensor(out=dst3, in0=src, in1=fac.rearrange("b (q t) -> b q t", t=4), op=MULT)
 
-        def tiles(m, order):
-            for i, h in order:
-                product(mx_tile(m, i, h), m, i, h)
-
-        def pair_order(j):
-            return ((2 * j, 0), (2 * j + 1, 0), (2 * j, 1), (2 * j + 1, 1))
-
-        def store_pair(m, j):
+        def store_half_pair(m, j, h):
             nc.sync.dma_start(
-                out=out_views[m][:, 2 * j : 2 * j + 2, :],
-                in_=o_sb[(m, j)][:].rearrange("p (c r) -> p c r", c=2),
+                out=out_views[m][:, 2 * j : 2 * j + 2, 512 * h : 512 * (h + 1)],
+                in_=o_sb[(m, j)][:].rearrange("p (c r) -> p c r", c=2)[:, :, 512 * h : 512 * (h + 1)],
             )
 
-        for h in range(2):
-            for t in range(4):
-                flip_y(0, h, t, t == 3)
-            quant_y(0, h, 0)
-            quant_y(0, h, 1)
-        for j in range(2):
-            flip_v(2 * j, False)
-            flip_v(2 * j + 1, True)
-            quant_v(j)
+        def store_row(m, i):
+            j, c = divmod(i, 2)
+            nc.sync.dma_start(out=out_views[m][:, i, :], in_=o_sb[(m, j)][:, 1024 * c : 1024 * (c + 1)])
 
-        tiles(0, pair_order(0))
-        store_pair(0, 0)
-        for i in range(4, 8):
-            flip_v(i, False)
-        quant_v(2)
-        tiles(0, pair_order(1))
-        store_pair(0, 1)
+        def store_tile(m, i, h):
+            j, c = divmod(i, 2)
+            lo = 1024 * c + 512 * h
+            nc.sync.dma_start(out=out_views[m][:, i, 512 * h : 512 * (h + 1)], in_=o_sb[(m, j)][:, lo : lo + 512])
+
         for t in range(4):
-            flip_y(1, 0, t, False)
-        quant_v(3)
-        tiles(0, pair_order(2))
-        store_pair(0, 2)
+            flip_y(0, 0, t)
+            quant_y_chunk(t)
+        for i in range(3):
+            flip_v(i)
+            quant_v_chunk(i)
+        flip_v(3)
+        tile_out(0, 0, 0)
+        quant_v_chunk(3)
+        tile_out(0, 1, 0)
+        store_half_pair(0, 0, 0)
+        flip_v(4)
+        flip_v(5)
+        tile_out(0, 2, 0)
+        quant_v_pair(2)
+        tile_out(0, 3, 0)
+        store_half_pair(0, 1, 0)
+        flip_v(6)
+        flip_v(7)
         for t in range(4):
-            flip_y(1, 1, t, False)
-        quant_y(1, 0, 0)
-        quant_y(1, 0, 1)
-        tiles(0, pair_order(3)[:2])
-        quant_y(1, 1, 0)
-        quant_y(1, 1, 1)
-        tiles(0, pair_order(3)[2:])
-        store_pair(0, 3)
-        for j in range(3):
-            tiles(1, pair_order(j))
-            store_pair(1, j)
-        tiles(1, ((6, 0), (6, 1)))
-        nc.sync.dma_start(out=out_views[1][:, 6, :], in_=o_sb[(1, 3)][:, 0:1024])
+            flip_y(0, 1, t)
+        quant_v_pair(3)
+        tile_out(0, 4, 0)
+        tile_out(0, 5, 0)
+        store_half_pair(0, 2, 0)
+        quant_y(0, 1)
+        tile_out(0, 6, 0)
+        tile_out(0, 7, 0)
+        store_half_pair(0, 3, 0)
+        for t in range(4):
+            flip_y(1, 0, t)
+        tile_out(0, 0, 1)
+        tile_out(0, 1, 1)
+        store_half_pair(0, 0, 1)
+        quant_y(1, 0)
+        tile_out(0, 2, 1)
+        tile_out(0, 3, 1)
+        store_half_pair(0, 1, 1)
+        for t in range(4):
+            flip_y(1, 1, t)
+        tile_out(0, 4, 1)
+        tile_out(0, 5, 1)
+        store_half_pair(0, 2, 1)
+        quant_y(1, 1)
+        tile_out(0, 6, 1)
+        tile_out(0, 7, 1)
+        store_half_pair(0, 3, 1)
+        for i in range(7):
+            tile_out(1, i, 0)
+            tile_out(1, i, 1)
+            store_row(1, i)
         for h in range(2):
-            tiles(1, ((7, h),))
-            nc.sync.dma_start(
-                out=out_views[1][:, 7, 512 * h : 512 * (h + 1)],
-                in_=o_sb[(1, 3)][:, 1024 + 512 * h : 1024 + 512 * (h + 1)],
-            )
+            tile_out(1, 7, h)
+            store_tile(1, 7, h)

@@ -32,6 +32,13 @@ def tile_pinnlayer_pb_kernel(tc, Volt, Y, Yconj, out_0, out_1):
 
         ident = keep.tile([P, P], F32, name="ident")
         make_identity(nc, ident[:])
+        zeros = keep.tile([P, 512], BF16, name="zeros")
+        nc.vector.memset(zeros[:], 0.0)
+
+        def warm(count):
+            for n in range(count):
+                w = acc_pool.tile([P, 512], F32, tag="acc", name="warm")
+                nc.tensor.matmul(out=w[:], lhsT=zeros[:, 0:P], rhs=zeros[:], start=True, stop=True)
 
         def load(view, rows, name):
             raw = keep.tile([P, rows * K], BF16, name=name)
@@ -135,7 +142,7 @@ def tile_pinnlayer_pb_kernel(tc, Volt, Y, Yconj, out_0, out_1):
 
         def tile_out(m, i, h):
             j, c = divmod(i, 2)
-            acc = acc_pool.tile([P, 512], F32)
+            acc = acc_pool.tile([P, 512], F32, tag="acc")
             for g in range(2):
                 lo = 256 * c + 128 * g
                 nc.tensor.matmul_mx(
@@ -173,13 +180,19 @@ def tile_pinnlayer_pb_kernel(tc, Volt, Y, Yconj, out_0, out_1):
             lo = 1024 * c + 512 * h
             nc.sync.dma_start(out=out_views[m][:, i, 512 * h : 512 * (h + 1)], in_=o_sb[(m, j)][:, lo : lo + 512])
 
+        warm(8)
         for t in range(4):
             flip_y(0, 0, t)
             quant_y_chunk(t)
+            if t % 2 == 1:
+                warm(1)
         for i in range(3):
             flip_v(i)
             quant_v_chunk(i)
+            if i == 1:
+                warm(1)
         flip_v(3)
+        warm(1)
         tile_out(0, 0, 0)
         quant_v_chunk(3)
         tile_out(0, 1, 0)

@@ -15,7 +15,7 @@ K = 1024
 KW = K // 2
 FLOPS = 2 * 2 * 1024 * 1024 * 1024
 
-OFFLOAD = ((1, 0, 0), (1, 2, 0), (1, 4, 0), (1, 6, 0))
+OFFLOAD = ((0, 2, 1), (0, 6, 1), (1, 0, 0), (1, 2, 0), (1, 4, 0), (1, 6, 0))
 
 
 def tile_pinnlayer_pb_kernel(tc, Volt, Y, Yconj, out_0, out_1):
@@ -122,12 +122,9 @@ def tile_pinnlayer_pb_kernel(tc, Volt, Y, Yconj, out_0, out_1):
                 )
 
         def quant_y(m, h):
-            for g in range(2):
-                nc.vector.quantize_mx(
-                    out=y_codes[(m, h)][:, 512 * g : 512 * (g + 1)].bitcast(FP8X4),
-                    scales=y_scales[(m, h)][:, 512 * g : 512 * (g + 1)],
-                    in_=y_grp[(m, h)][:, 2048 * g : 2048 * (g + 1)],
-                )
+            nc.vector.quantize_mx(
+                out=y_codes[(m, h)][:].bitcast(FP8X4), scales=y_scales[(m, h)][:], in_=y_grp[(m, h)][:]
+            )
 
         def quant_v_chunk(i):
             j, c = divmod(i, 2)
@@ -218,18 +215,18 @@ def tile_pinnlayer_pb_kernel(tc, Volt, Y, Yconj, out_0, out_1):
         for t in range(4):
             flip_y(1, 0, t)
         tile_out(0, 0, 1)
+        quant_y(1, 0)
         tile_out(0, 1, 1)
         store_half_pair(0, 0, 1)
-        quant_y(1, 0)
         tile_out(0, 2, 1)
         tile_out(0, 3, 1)
         store_half_pair(0, 1, 1)
         for t in range(4):
             flip_y(1, 1, t)
         tile_out(0, 4, 1)
+        quant_y(1, 1)
         tile_out(0, 5, 1)
         store_half_pair(0, 2, 1)
-        quant_y(1, 1)
         tile_out(0, 6, 1)
         tile_out(0, 7, 1)
         store_half_pair(0, 3, 1)

@@ -15,7 +15,7 @@ K = 1024
 KW = K // 2
 FLOPS = 2 * 2 * 1024 * 1024 * 1024
 
-OFFLOAD = ((0, 2, 1), (0, 6, 1), (1, 0, 0), (1, 2, 0), (1, 4, 0), (1, 6, 0))
+OFFLOAD = ((1, 0, 0), (1, 2, 0), (1, 4, 0), (1, 6, 0))
 
 
 def tile_pinnlayer_pb_kernel(tc, Volt, Y, Yconj, out_0, out_1):
@@ -46,13 +46,16 @@ def tile_pinnlayer_pb_kernel(tc, Volt, Y, Yconj, out_0, out_1):
             return raw
 
         def load_half(m, h, pieces):
-            view = mats[m][512 * h : 512 * (h + 1), :].rearrange("(q t) k -> q t k", t=4)
-            per = 4 // pieces
+            view = mats[m][512 * h : 512 * (h + 1), :].rearrange("(s q t) k -> q s (t k)", s=2, t=2)
+            per = 2 // pieces
             chunks = []
-            for s in range(pieces):
-                raw = load(view[:, per * s : per * (s + 1), :], per, "yraw%d%d%d" % (m, h, s))
+            for n in range(pieces):
+                raw = keep.tile([P, 2 * per * K], BF16, name="yraw%d%d%d" % (m, h, n))
+                nc.sync.dma_start(
+                    out=raw[:].rearrange("p (s x) -> p s x", s=per), in_=view[:, per * n : per * (n + 1), :]
+                )
                 words = raw[:].bitcast(F32)
-                for t in range(per):
+                for t in range(2 * per):
                     chunks.append(words[:, KW * t : KW * (t + 1)])
             return chunks
 
@@ -122,9 +125,12 @@ def tile_pinnlayer_pb_kernel(tc, Volt, Y, Yconj, out_0, out_1):
                 )
 
         def quant_y(m, h):
-            nc.vector.quantize_mx(
-                out=y_codes[(m, h)][:].bitcast(FP8X4), scales=y_scales[(m, h)][:], in_=y_grp[(m, h)][:]
-            )
+            for g in range(2):
+                nc.vector.quantize_mx(
+                    out=y_codes[(m, h)][:, 512 * g : 512 * (g + 1)].bitcast(FP8X4),
+                    scales=y_scales[(m, h)][:, 512 * g : 512 * (g + 1)],
+                    in_=y_grp[(m, h)][:, 2048 * g : 2048 * (g + 1)],
+                )
 
         def quant_v_chunk(i):
             j, c = divmod(i, 2)
@@ -154,13 +160,13 @@ def tile_pinnlayer_pb_kernel(tc, Volt, Y, Yconj, out_0, out_1):
             lo = 1024 * c + 512 * h
             dst = o_sb[(m, j)][:, lo : lo + 512]
             fac = v_raw[j][:, lo : lo + 512]
-            src = acc[:].rearrange("b (t q) -> b q t", t=4)
-            dst3 = dst.rearrange("b (q t) -> b q t", t=4)
+            src = acc[:].rearrange("b (s t q) -> b s q t", s=2, t=2)
+            dst3 = dst.rearrange("b (s q t) -> b s q t", s=2, t=2)
             if (m, i, h) in OFFLOAD:
                 nc.scalar.copy(out=dst3, in_=src)
                 nc.gpsimd.tensor_tensor(out=dst, in0=dst, in1=fac, op=MULT)
             else:
-                nc.vector.tensor_tensor(out=dst3, in0=src, in1=fac.rearrange("b (q t) -> b q t", t=4), op=MULT)
+                nc.vector.tensor_tensor(out=dst3, in0=src, in1=fac.rearrange("b (s q t) -> b s q t", s=2, t=2), op=MULT)
 
         def store_half_pair(m, j, h):
             nc.sync.dma_start(
@@ -215,18 +221,18 @@ def tile_pinnlayer_pb_kernel(tc, Volt, Y, Yconj, out_0, out_1):
         for t in range(4):
             flip_y(1, 0, t)
         tile_out(0, 0, 1)
-        quant_y(1, 0)
         tile_out(0, 1, 1)
         store_half_pair(0, 0, 1)
+        quant_y(1, 0)
         tile_out(0, 2, 1)
         tile_out(0, 3, 1)
         store_half_pair(0, 1, 1)
         for t in range(4):
             flip_y(1, 1, t)
         tile_out(0, 4, 1)
-        quant_y(1, 1)
         tile_out(0, 5, 1)
         store_half_pair(0, 2, 1)
+        quant_y(1, 1)
         tile_out(0, 6, 1)
         tile_out(0, 7, 1)
         store_half_pair(0, 3, 1)

from contextlib import ExitStack

import concourse.mybir as mybir
from concourse.masks import make_identity

F32 = mybir.dt.float32
BF16 = mybir.dt.bfloat16
U32 = mybir.dt.uint32
U8 = mybir.dt.uint8
FP8X4 = mybir.dt.float8_e4m3fn_x4
MULT = mybir.AluOpType.mult

P = 128
K = 1024
KW = K // 2
FLOPS = 2 * 2 * 1024 * 1024 * 1024

OFFLOAD = ((1, 0, 0), (1, 2, 0), (1, 4, 0), (1, 6, 0))


def tile_pinnlayer_pb_kernel(tc, Volt, Y, Yconj, out_0, out_1):
    nc = tc.nc
    mats = (Y, Yconj)
    out_views = tuple(o.rearrange("(p t) r -> p t r", t=8) for o in (out_0, out_1))
    volt_view = Volt.rearrange("(p t) k -> p t k", t=8)

    with ExitStack() as ctx:
        keep = ctx.enter_context(tc.tile_pool(name="keep", bufs=1))
        tp_pool = ctx.enter_context(tc.psum_pool(name="tp", bufs=4))
        acc_pool = ctx.enter_context(tc.psum_pool(name="acc", bufs=4))
        ctx.enter_context(tc.manual_schedule())

        ident = keep.tile([P, P], F32, name="ident")
        make_identity(nc, ident[:])
        zeros = keep.tile([P, 512], BF16, name="zeros")
        nc.vector.memset(zeros[:], 0.0)

        def warm(count):
            for n in range(count):
                w = acc_pool.tile([P, 512], F32, tag="acc", name="warm")
                nc.tensor.matmul(out=w[:], lhsT=zeros[:, 0:P], rhs=zeros[:], start=True, stop=True)

        def load(view, rows, name):
            raw = keep.tile([P, rows * K], BF16, name=name)
            nc.sync.dma_start(out=raw[:].rearrange("p (t k) -> p t k", t=rows), in_=view)
            return raw

        def load_half(m, h, pieces):
            view = mats[m][512 * h : 512 * (h + 1), :].rearrange("(s q t) k -> q s (t k)", s=2, t=2)
            per = 2 // pieces
            chunks = []
            for n in range(pieces):
                raw = keep.tile([P, 2 * per * K], BF16, name="yraw%d%d%d" % (m, h, n))
                nc.sync.dma_start(
                    out=raw[:].rearrange("p (s x) -> p s x", s=per), in_=view[:, per * n : per * (n + 1), :]
                )
                words = raw[:].bitcast(F32)
                for t in range(2 * per):
                    chunks.append(words[:, KW * t : KW * (t + 1)])
            return chunks

        y_chunks = {}
        v_raw = []
        y_chunks[(0, 0)] = load_half(0, 0, 2)
        for j in range(4):
            v_raw.append(load(volt_view[:, 2 * j : 2 * j + 2, :], 2, "vraw%d" % j))
        y_chunks[(0, 1)] = load_half(0, 1, 1)
        y_chunks[(1, 0)] = load_half(1, 0, 1)
        y_chunks[(1, 1)] = load_half(1, 1, 1)

        y_grp = {}
        y_codes = {}
        y_scales = {}
        for m in range(2):
            for h in range(2):
                if (m, h) == (0, 0):
                    for t in range(4):
                        y_grp[(m, h, t)] = keep.tile([P, 1024], BF16, name="ygrp%d%d%d" % (m, h, t), align_bytes=64)
                else:
                    y_grp[(m, h)] = keep.tile([P, 4096], BF16, name="ygrp%d%d" % (m, h), align_bytes=64)
                y_codes[(m, h)] = keep.tile([P, 1024], U32, name="ycod%d%d" % (m, h), align_bytes=64)
                y_scales[(m, h)] = keep.tile([P, 1024], U8, name="yscl%d%d" % (m, h), align_bytes=64)
        v_grp = {}
        v_codes = []
        v_scales = []
        o_sb = {}
        for i in range(4):
            v_grp[i] = keep.tile([P, 1024], BF16, name="vgrpc%d" % i, align_bytes=64)
        for j in range(4):
            if j >= 2:
                v_grp[(j,)] = keep.tile([P, 2048], BF16, name="vgrpp%d" % j, align_bytes=64)
            v_codes.append(keep.tile([P, 512], U32, name="vcod%d" % j, align_bytes=64))
            v_scales.append(keep.tile([P, 512], U8, name="vscl%d" % j, align_bytes=64))
            for m in range(2):
                o_sb[(m, j)] = keep.tile([P, 2048], F32, name="osb%d%d" % (m, j))

        def flip(words, dest):
            ps = tp_pool.tile([P, 4, P], F32)
            for w in range(4):
                nc.tensor.transpose(ps[:, w, :], words[:, P * w : P * (w + 1)], ident[:])
            nc.scalar.copy(out=dest, in_=ps[:].rearrange("p (g u) r -> p g r u", g=2))

        def flip_y(m, h, t):
            if (m, h) == (0, 0):
                dest = y_grp[(m, h, t)][:].bitcast(F32).rearrange("p (g q u) -> p g q u", g=2, u=2)
            else:
                dest = y_grp[(m, h)][:].bitcast(F32).rearrange("p (g t q u) -> p g t q u", g=2, t=4, u=2)[:, :, t, :, :]
            flip(y_chunks[(m, h)][t], dest)

        def flip_v(i):
            j, c = divmod(i, 2)
            if i < 4:
                dest = v_grp[i][:].bitcast(F32).rearrange("p (g b u) -> p g b u", g=2, u=2)
            else:
                dest = v_grp[(j,)][:].bitcast(F32).rearrange("p (c g b u) -> p c g b u", c=2, g=2, u=2)[:, c, :, :, :]
            flip(v_raw[j][:].bitcast(F32)[:, KW * c : KW * (c + 1)], dest)

        def quant_y_chunk(t):
            for g in range(2):
                lo = 512 * g + 128 * t
                nc.vector.quantize_mx(
                    out=y_codes[(0, 0)][:, lo : lo + 128].bitcast(FP8X4),
                    scales=y_scales[(0, 0)][:, lo : lo + 128],
                    in_=y_grp[(0, 0, t)][:, 512 * g : 512 * (g + 1)],
                )

        def quant_y(m, h):
            for g in range(2):
                nc.vector.quantize_mx(
                    out=y_codes[(m, h)][:, 512 * g : 512 * (g + 1)].bitcast(FP8X4),
                    scales=y_scales[(m, h)][:, 512 * g : 512 * (g + 1)],
                    in_=y_grp[(m, h)][:, 2048 * g : 2048 * (g + 1)],
                )

        def quant_v_chunk(i):
            j, c = divmod(i, 2)
            nc.vector.quantize_mx(
                out=v_codes[j][:, 256 * c : 256 * (c + 1)].bitcast(FP8X4),
                scales=v_scales[j][:, 256 * c : 256 * (c + 1)],
                in_=v_grp[i][:],
            )

        def quant_v_pair(j):
            nc.vector.quantize_mx(out=v_codes[j][:].bitcast(FP8X4), scales=v_scales[j][:], in_=v_grp[(j,)][:])

        def tile_out(m, i, h):
            j, c = divmod(i, 2)
            acc = acc_pool.tile([P, 512], F32, tag="acc")
            for g in range(2):
                lo = 256 * c + 128 * g
                nc.tensor.matmul_mx(
                    out=acc[:],
                    lhsT=v_codes[j][:, lo : lo + 128].bitcast(FP8X4),
                    lhsT_scale=v_scales[j][:, lo : lo + 128],
                    rhs=y_codes[(m, h)][:, 512 * g : 512 * (g + 1)].bitcast(FP8X4),
                    rhs_scale=y_scales[(m, h)][:, 512 * g : 512 * (g + 1)],
                    start=(g == 0),
                    stop=(g == 1),
                )
            lo = 1024 * c + 512 * h
            dst = o_sb[(m, j)][:, lo : lo + 512]
            fac = v_raw[j][:, lo : lo + 512]
            src = acc[:].rearrange("b (s t q) -> b s q t", s=2, t=2)
            dst3 = dst.rearrange("b (s q t) -> b s q t", s=2, t=2)
            if (m, i, h) in OFFLOAD:
                nc.scalar.copy(out=dst3, in_=src)
                nc.gpsimd.tensor_tensor(out=dst, in0=dst, in1=fac, op=MULT)
            else:
                nc.vector.tensor_tensor(out=dst3, in0=src, in1=fac.rearrange("b (s q t) -> b s q t", s=2, t=2), op=MULT)

        def store_half_pair(m, j, h):
            nc.sync.dma_start(
                out=out_views[m][:, 2 * j : 2 * j + 2, 512 * h : 512 * (h + 1)],
                in_=o_sb[(m, j)][:].rearrange("p (c r) -> p c r", c=2)[:, :, 512 * h : 512 * (h + 1)],
            )

        def store_row(m, i):
            j, c = divmod(i, 2)
            nc.sync.dma_start(out=out_views[m][:, i, :], in_=o_sb[(m, j)][:, 1024 * c : 1024 * (c + 1)])

        def store_tile(m, i, h):
            j, c = divmod(i, 2)
            lo = 1024 * c + 512 * h
            nc.sync.dma_start(out=out_views[m][:, i, 512 * h : 512 * (h + 1)], in_=o_sb[(m, j)][:, lo : lo + 512])

        warm(8)
        for t in range(4):
            flip_y(0, 0, t)
            quant_y_chunk(t)
            if t % 2 == 1:
                warm(1)
        for i in range(3):
            flip_v(i)
            quant_v_chunk(i)
            if i == 1:
                warm(1)
        flip_v(3)
        warm(1)
        tile_out(0, 0, 0)
        quant_v_chunk(3)
        tile_out(0, 1, 0)
        store_half_pair(0, 0, 0)
        flip_v(4)
        flip_v(5)
        tile_out(0, 2, 0)
        quant_v_pair(2)
        tile_out(0, 3, 0)
        store_half_pair(0, 1, 0)
        flip_v(6)
        flip_v(7)
        for t in range(4):
            flip_y(0, 1, t)
        quant_v_pair(3)
        tile_out(0, 4, 0)
        tile_out(0, 5, 0)
        store_half_pair(0, 2, 0)
        quant_y(0, 1)
        tile_out(0, 6, 0)
        tile_out(0, 7, 0)
        store_half_pair(0, 3, 0)
        for t in range(4):
            flip_y(1, 0, t)
        tile_out(0, 0, 1)
        tile_out(0, 1, 1)
        store_half_pair(0, 0, 1)
        quant_y(1, 0)
        tile_out(0, 2, 1)
        tile_out(0, 3, 1)
        store_half_pair(0, 1, 1)
        for t in range(4):
            flip_y(1, 1, t)
        tile_out(0, 4, 1)
        tile_out(0, 5, 1)
        store_half_pair(0, 2, 1)
        quant_y(1, 1)
        tile_out(0, 6, 1)
        tile_out(0, 7, 1)
        store_half_pair(0, 3, 1)
        for i in range(7):
            tile_out(1, i, 0)
            tile_out(1, i, 1)
            store_row(1, i)
        for h in range(2):
            tile_out(1, 7, h)
            store_tile(1, 7, h)
